import numpy as np
import ml_dtypes


def mxq(x, axis, fmt="e4m3"):
    dtype, down = {"e4m3": (ml_dtypes.float8_e4m3fn, 7), "e5m2": (ml_dtypes.float8_e5m2, 14)}[fmt]
    v = np.moveaxis(np.asarray(x, np.float32).astype(ml_dtypes.bfloat16).astype(np.float64), axis, -1)
    blocks = v.reshape(v.shape[:-1] + (-1, 32))
    amax = np.abs(blocks).max(-1, keepdims=True)
    byte = np.maximum(np.where(amax > 0, np.frexp(amax)[1] - 1 + 127, 0) - down, 1)
    scale = np.exp2(byte - 127.0)
    codes = (blocks / scale).astype(np.float32).astype(dtype).astype(np.float64)
    return np.moveaxis((codes * scale).reshape(v.shape), -1, axis)


WIDE = False


def mx_kscale(k):
    if not WIDE:
        return np.ones(k)
    levels = np.array([20, -20, 10, -10, 0])
    a = np.random.permutation(np.resize(levels, k // 512 * 4)).reshape(k // 512, 4)
    idx = np.arange(k)
    return np.exp2(a[idx // 512, idx % 128 // 32])


BF16 = ml_dtypes.bfloat16


def bf(x):
    return np.asarray(x, np.float32).astype(BF16)


def f64(x):
    return np.asarray(x).astype(np.float64)


B, A, C, P = 8192, 1, 512, 512
N = A * A + 1
T = B * N


def scramble(y):
    return y.transpose(0, 2, 1).reshape(B, N, C)


def unscramble(z):
    return z.reshape(B, C, N).transpose(0, 2, 1)


def setup_inputs():
    s = mx_kscale(T).reshape(B, N, 1)
    z = np.random.standard_normal((B, N, C)) * 1.6 / np.sqrt(N) * s
    w = np.random.standard_normal((P, C)) * 2.0 / np.sqrt(C)
    b = np.random.standard_normal(P) * 0.1
    g = np.random.standard_normal((B, N, P)) * np.exp2(np.random.randint(-12, 1, (B, N, 1))) / s
    return {"y_attn": bf(np.ascontiguousarray(unscramble(z))),
            "w_proj": bf(w),
            "b_proj": bf(b),
            "grad_out": bf(g)}


def reference(y_attn, w_proj, b_proj, grad_out):
    z = scramble(f64(y_attn)).reshape(T, C)
    g = f64(grad_out).reshape(T, P)
    return mxq(g, 0, "e5m2").T @ mxq(z, 0, "e4m3")

@@ -1,0 +1,113 @@
+import concourse.mybir as mybir
+
+FLOPS = 2 * 16384 * 512 * 512
+BYTES = 2 * 16384 * 512 * 2 + 512 * 512 * 4
+
+BF16 = mybir.dt.bfloat16
+F32 = mybir.dt.float32
+U32 = mybir.dt.uint32
+U8 = mybir.dt.uint8
+E4M3_X4 = mybir.dt.float8_e4m3fn_x4
+E5M2_X4 = mybir.dt.float8_e5m2_x4
+
+P = 128
+PACK = 4
+K_PASS = P * PACK
+IMAGES = 8192
+TOKENS = 2
+WIDTH = 512
+HALF = WIDTH // TOKENS
+PASSES = IMAGES * TOKENS // K_PASS
+IMAGES_PER_PARTITION = PACK // TOKENS
+M_TILE = 128
+M_TILES = WIDTH // M_TILE
+RUN = 4
+
+RAW_BUFS = 8
+WORK_BUFS = 3
+
+
+def tile_attention_pa_k_kernel(tc, y_attn, w_proj, b_proj, grad_out, out):
+    nc = tc.nc
+
+    g_passes = grad_out.rearrange("(k p h) i w -> k p (h i w)", p=P, h=IMAGES_PER_PARTITION)
+    y_passes = y_attn.rearrange("(k p h) n w -> k p (h n w)", p=P, h=IMAGES_PER_PARTITION)
+
+    with tc.tile_pool(name="raw", bufs=RAW_BUFS) as raw, tc.tile_pool(
+        name="work", bufs=WORK_BUFS
+    ) as work, tc.tile_pool(name="result", bufs=1) as result, tc.psum_pool(
+        name="psum", bufs=1
+    ) as psum, tc.manual_schedule():
+        acc = [psum.tile([M_TILE, WIDTH], F32, name="acc%d" % m) for m in range(M_TILES)]
+        g_operands = {}
+        z_operands = {}
+        grouped = {}
+
+        def load_and_regroup(k):
+            y_raw = raw.tile([P, IMAGES_PER_PARTITION, TOKENS, TOKENS, HALF], BF16)
+            nc.sync.dma_start(out=y_raw[:].rearrange("p h n i c -> p (h n i c)"), in_=y_passes[k])
+            g_raw = raw.tile([P, PACK, WIDTH], BF16)
+            nc.sync.dma_start(out=g_raw[:].rearrange("p j w -> p (j w)"), in_=g_passes[k])
+
+            z_grouped = work.tile([P, TOKENS, HALF, PACK], BF16, align_bytes=64)
+            for n in range(TOKENS):
+                nc.vector.tensor_copy(
+                    out=z_grouped[:, n].rearrange("p (c r) (h i) -> p c h i r", r=RUN, i=TOKENS),
+                    in_=y_raw[:, :, n].rearrange("p h i (c r) -> p c h i r", r=RUN),
+                )
+            g_grouped = work.tile([P, WIDTH, PACK], BF16, align_bytes=64)
+            nc.scalar.copy(
+                out=g_grouped[:].rearrange("p (c r) j -> p c j r", r=RUN),
+                in_=g_raw[:].rearrange("p j (c r) -> p c j r", r=RUN),
+            )
+            grouped[k] = (z_grouped, g_grouped)
+
+        def quantise(k):
+            z_grouped, g_grouped = grouped.pop(k)
+            z_codes = work.tile([P, WIDTH], U32, align_bytes=64)
+            z_scales = work.tile([P, WIDTH], U8, align_bytes=64)
+            nc.vector.quantize_mx(
+                out=z_codes[:].bitcast(E4M3_X4),
+                scales=z_scales[:],
+                in_=z_grouped[:].rearrange("p n c j -> p (n c j)"),
+            )
+            g_codes = work.tile([P, WIDTH], U32, align_bytes=64)
+            g_scales = work.tile([P, WIDTH], U8, align_bytes=64)
+            nc.vector.quantize_mx(
+                out=g_codes[:].bitcast(E5M2_X4),
+                scales=g_scales[:],
+                in_=g_grouped[:].rearrange("p w j -> p (w j)"),
+            )
+            z_operands[k] = (z_codes, z_scales)
+            g_operands[k] = (g_codes, g_scales)
+
+        def multiply(k):
+            z_codes, z_scales = z_operands.pop(k)
+            g_codes, g_scales = g_operands.pop(k)
+            for m in range(M_TILES):
+                m_cols = slice(m * M_TILE, (m + 1) * M_TILE)
+                nc.tensor.matmul_mx(
+                    out=acc[m][:],
+                    lhsT=g_codes[:, m_cols].bitcast(E5M2_X4),
+                    lhsT_scale=g_scales[:, m_cols],
+                    rhs=z_codes[:].bitcast(E4M3_X4),
+                    rhs_scale=z_scales[:],
+                    start=(k == 0),
+                    stop=(k == PASSES - 1),
+                )
+
+        for k in range(PASSES + 1):
+            if k < PASSES:
+                load_and_regroup(k)
+            if k > 0:
+                quantise(k - 1)
+                multiply(k - 1)
+
+        for m in range(M_TILES):
+            out_rows = result.tile([M_TILE, HALF, TOKENS], F32, name="out_rows%d" % m)
+            copy_engine = nc.vector.tensor_copy if m % 2 == 0 else nc.scalar.copy
+            copy_engine(out=out_rows[:], in_=acc[m][:].rearrange("p (n c) -> p c n", n=TOKENS))
+            nc.sync.dma_start(
+                out=out[m * M_TILE : (m + 1) * M_TILE, :],
+                in_=out_rows[:].rearrange("p c n -> p (c n)"),
+            )

@@ -1,4 +1,5 @@
 import concourse.mybir as mybir
+from concourse.masks import make_identity
 
 FLOPS = 2 * 16384 * 512 * 512
 BYTES = 2 * 16384 * 512 * 2 + 512 * 512 * 4
@@ -23,6 +24,10 @@ M_TILE = 128
 M_TILES = WIDTH // M_TILE
 RUN = 4
 
+PE_COLS = 192
+PE_SPLIT = 2
+STAGE_BUFS = 3
+
 RAW_BUFS = 8
 WORK_BUFS = 3
 
@@ -37,7 +42,9 @@ def tile_attention_pa_k_kernel(tc, y_attn, w_proj, b_proj, grad_out, out):
         name="work", bufs=WORK_BUFS
     ) as work, tc.tile_pool(name="result", bufs=1) as result, tc.psum_pool(
         name="psum", bufs=1
-    ) as psum, tc.manual_schedule():
+    ) as psum, tc.psum_pool(name="stage", bufs=STAGE_BUFS) as stage, tc.manual_schedule():
+        ident = result.tile([P, P], BF16, name="ident")
+        make_identity(nc, ident[:])
         acc = [psum.tile([M_TILE, WIDTH], F32, name="acc%d" % m) for m in range(M_TILES)]
         g_operands = {}
         z_operands = {}
@@ -56,10 +63,21 @@ def tile_attention_pa_k_kernel(tc, y_attn, w_proj, b_proj, grad_out, out):
                     in_=y_raw[:, :, n].rearrange("p h i (c r) -> p c h i r", r=RUN),
                 )
             g_grouped = work.tile([P, WIDTH, PACK], BF16, align_bytes=64)
+            g_bank = stage.tile([P, PE_COLS, PACK], BF16)
+            step = PE_COLS // PE_SPLIT
+            for s in range(PE_SPLIT):
+                nc.tensor.matmul(
+                    out=g_bank[:, s * step : (s + 1) * step, :],
+                    lhsT=ident[:],
+                    rhs=g_raw[:, :, s * step : (s + 1) * step].rearrange("p j c -> p c j"),
+                    start=True,
+                    stop=True,
+                )
             nc.scalar.copy(
-                out=g_grouped[:].rearrange("p (c r) j -> p c j r", r=RUN),
-                in_=g_raw[:].rearrange("p j (c r) -> p c j r", r=RUN),
+                out=g_grouped[:, PE_COLS:, :].rearrange("p (c r) j -> p c j r", r=RUN),
+                in_=g_raw[:, :, PE_COLS:].rearrange("p j (c r) -> p c j r", r=RUN),
             )
+            nc.scalar.copy(out=g_grouped[:, :PE_COLS, :], in_=g_bank[:])
             grouped[k] = (z_grouped, g_grouped)
 
         def quantise(k):

@@ -26,6 +26,7 @@ RUN = 4
 
 PE_COLS = 192
 PE_SPLIT = 2
+Z_SCALAR_COLS = 64
 STAGE_BUFS = 3
 
 RAW_BUFS = 8
@@ -58,10 +59,15 @@ def tile_attention_pa_k_kernel(tc, y_attn, w_proj, b_proj, grad_out, out):
 
             z_grouped = work.tile([P, TOKENS, HALF, PACK], BF16, align_bytes=64)
             for n in range(TOKENS):
+                vector_cols = HALF if n == 0 else HALF - Z_SCALAR_COLS
                 nc.vector.tensor_copy(
-                    out=z_grouped[:, n].rearrange("p (c r) (h i) -> p c h i r", r=RUN, i=TOKENS),
-                    in_=y_raw[:, :, n].rearrange("p h i (c r) -> p c h i r", r=RUN),
+                    out=z_grouped[:, n, :vector_cols].rearrange("p (c r) (h i) -> p c h i r", r=RUN, i=TOKENS),
+                    in_=y_raw[:, :, n, :, :vector_cols].rearrange("p h i (c r) -> p c h i r", r=RUN),
                 )
+            nc.scalar.copy(
+                out=z_grouped[:, 1, HALF - Z_SCALAR_COLS :].rearrange("p (c r) (h i) -> p c h i r", r=RUN, i=TOKENS),
+                in_=y_raw[:, :, 1, :, HALF - Z_SCALAR_COLS :].rearrange("p h i (c r) -> p c h i r", r=RUN),
+            )
             g_grouped = work.tile([P, WIDTH, PACK], BF16, align_bytes=64)
             g_bank = stage.tile([P, PE_COLS, PACK], BF16)
             step = PE_COLS // PE_SPLIT

@@ -27,6 +27,7 @@ RUN = 4
 PE_COLS = 192
 PE_SPLIT = 2
 Z_SCALAR_COLS = 64
+LAST_ORDER = (2, 3, 0, 1)
 STAGE_BUFS = 3
 
 RAW_BUFS = 8
@@ -49,14 +50,12 @@ def tile_attention_pa_k_kernel(tc, y_attn, w_proj, b_proj, grad_out, out):
         acc = [psum.tile([M_TILE, WIDTH], F32, name="acc%d" % m) for m in range(M_TILES)]
         g_operands = {}
         z_operands = {}
-        grouped = {}
+        z_grouped_of = {}
+        g_grouped_of = {}
 
-        def load_and_regroup(k):
+        def regroup_z(k):
             y_raw = raw.tile([P, IMAGES_PER_PARTITION, TOKENS, TOKENS, HALF], BF16)
             nc.sync.dma_start(out=y_raw[:].rearrange("p h n i c -> p (h n i c)"), in_=y_passes[k])
-            g_raw = raw.tile([P, PACK, WIDTH], BF16)
-            nc.sync.dma_start(out=g_raw[:].rearrange("p j w -> p (j w)"), in_=g_passes[k])
-
             z_grouped = work.tile([P, TOKENS, HALF, PACK], BF16, align_bytes=64)
             for n in range(TOKENS):
                 vector_cols = HALF if n == 0 else HALF - Z_SCALAR_COLS
@@ -68,6 +67,17 @@ def tile_attention_pa_k_kernel(tc, y_attn, w_proj, b_proj, grad_out, out):
                 out=z_grouped[:, 1, HALF - Z_SCALAR_COLS :].rearrange("p (c r) (h i) -> p c h i r", r=RUN, i=TOKENS),
                 in_=y_raw[:, :, 1, :, HALF - Z_SCALAR_COLS :].rearrange("p h i (c r) -> p c h i r", r=RUN),
             )
+            z_grouped_of[k] = z_grouped
+
+        def strided_g(copy, g_grouped, g_raw, cols):
+            copy(
+                out=g_grouped[:, cols, :].rearrange("p (c r) j -> p c j r", r=RUN),
+                in_=g_raw[:, :, cols].rearrange("p j (c r) -> p c j r", r=RUN),
+            )
+
+        def regroup_g(k):
+            g_raw = raw.tile([P, PACK, WIDTH], BF16)
+            nc.sync.dma_start(out=g_raw[:].rearrange("p j w -> p (j w)"), in_=g_passes[k])
             g_grouped = work.tile([P, WIDTH, PACK], BF16, align_bytes=64)
             g_bank = stage.tile([P, PE_COLS, PACK], BF16)
             step = PE_COLS // PE_SPLIT
@@ -79,15 +89,16 @@ def tile_attention_pa_k_kernel(tc, y_attn, w_proj, b_proj, grad_out, out):
                     start=True,
                     stop=True,
                 )
-            nc.scalar.copy(
-                out=g_grouped[:, PE_COLS:, :].rearrange("p (c r) j -> p c j r", r=RUN),
-                in_=g_raw[:, :, PE_COLS:].rearrange("p j (c r) -> p c j r", r=RUN),
-            )
+            if k < PASSES - 1:
+                strided_g(nc.scalar.copy, g_grouped, g_raw, slice(PE_COLS, WIDTH))
+            else:
+                for m in LAST_ORDER[:2]:
+                    strided_g(nc.scalar.copy, g_grouped, g_raw, slice(m * M_TILE, (m + 1) * M_TILE))
             nc.scalar.copy(out=g_grouped[:, :PE_COLS, :], in_=g_bank[:])
-            grouped[k] = (z_grouped, g_grouped)
+            g_grouped_of[k] = (g_grouped, g_raw)
 
-        def quantise(k):
-            z_grouped, g_grouped = grouped.pop(k)
+        def quantise_z(k):
+            z_grouped = z_grouped_of.pop(k)
             z_codes = work.tile([P, WIDTH], U32, align_bytes=64)
             z_scales = work.tile([P, WIDTH], U8, align_bytes=64)
             nc.vector.quantize_mx(
@@ -95,43 +106,62 @@ def tile_attention_pa_k_kernel(tc, y_attn, w_proj, b_proj, grad_out, out):
                 scales=z_scales[:],
                 in_=z_grouped[:].rearrange("p n c j -> p (n c j)"),
             )
-            g_codes = work.tile([P, WIDTH], U32, align_bytes=64)
-            g_scales = work.tile([P, WIDTH], U8, align_bytes=64)
-            nc.vector.quantize_mx(
-                out=g_codes[:].bitcast(E5M2_X4),
-                scales=g_scales[:],
-                in_=g_grouped[:].rearrange("p w j -> p (w j)"),
-            )
             z_operands[k] = (z_codes, z_scales)
-            g_operands[k] = (g_codes, g_scales)
 
-        def multiply(k):
-            z_codes, z_scales = z_operands.pop(k)
-            g_codes, g_scales = g_operands.pop(k)
-            for m in range(M_TILES):
-                m_cols = slice(m * M_TILE, (m + 1) * M_TILE)
-                nc.tensor.matmul_mx(
-                    out=acc[m][:],
-                    lhsT=g_codes[:, m_cols].bitcast(E5M2_X4),
-                    lhsT_scale=g_scales[:, m_cols],
-                    rhs=z_codes[:].bitcast(E4M3_X4),
-                    rhs_scale=z_scales[:],
-                    start=(k == 0),
-                    stop=(k == PASSES - 1),
-                )
-
-        for k in range(PASSES + 1):
-            if k < PASSES:
-                load_and_regroup(k)
-            if k > 0:
-                quantise(k - 1)
-                multiply(k - 1)
-
-        for m in range(M_TILES):
-            out_rows = result.tile([M_TILE, HALF, TOKENS], F32, name="out_rows%d" % m)
-            copy_engine = nc.vector.tensor_copy if m % 2 == 0 else nc.scalar.copy
-            copy_engine(out=out_rows[:], in_=acc[m][:].rearrange("p (n c) -> p c n", n=TOKENS))
-            nc.sync.dma_start(
-                out=out[m * M_TILE : (m + 1) * M_TILE, :],
-                in_=out_rows[:].rearrange("p c n -> p (c n)"),
+        def quantise_g(k, cols):
+            if k not in g_operands:
+                g_codes = work.tile([P, WIDTH], U32, align_bytes=64)
+                g_scales = work.tile([P, WIDTH], U8, align_bytes=64)
+                g_operands[k] = (g_codes, g_scales)
+            g_codes, g_scales = g_operands[k]
+            nc.vector.quantize_mx(
+                out=g_codes[:, cols].bitcast(E5M2_X4),
+                scales=g_scales[:, cols],
+                in_=g_grouped_of[k][0][:, cols, :].rearrange("p w j -> p (w j)"),
             )
+
+        def multiply(k, m):
+            z_codes, z_scales = z_operands[k]
+            g_codes, g_scales = g_operands[k]
+            m_cols = slice(m * M_TILE, (m + 1) * M_TILE)
+            nc.tensor.matmul_mx(
+                out=acc[m][:],
+                lhsT=g_codes[:, m_cols].bitcast(E5M2_X4),
+                lhsT_scale=g_scales[:, m_cols],
+                rhs=z_codes[:].bitcast(E4M3_X4),
+                rhs_scale=z_scales[:],
+                start=(k == 0),
+                stop=(k == PASSES - 1),
+            )
+
+        for k in range(PASSES):
+            regroup_z(k)
+            regroup_g(k)
+            if k > 0:
+                quantise_g(k - 1, slice(0, WIDTH))
+                for m in range(M_TILES):
+                    multiply(k - 1, m)
+            quantise_z(k)
+
+        last = PASSES - 1
+        g_grouped, g_raw = g_grouped_of[last]
+        strided_g(nc.vector.tensor_copy, g_grouped, g_raw, slice(PE_COLS, 2 * M_TILE))
+        for m in LAST_ORDER:
+            quantise_g(last, slice(m * M_TILE, (m + 1) * M_TILE))
+            multiply(last, m)
+
+        for place, m in enumerate(LAST_ORDER):
+            out_rows = result.tile([M_TILE, HALF, TOKENS], F32, name="out_rows%d" % m)
+            copy_engine = nc.vector.tensor_copy if place % 2 == 0 else nc.scalar.copy
+            pieces = 2 if place == M_TILES - 1 else 1
+            width = HALF // pieces
+            for piece in range(pieces):
+                c_range = slice(piece * width, (piece + 1) * width)
+                copy_engine(
+                    out=out_rows[:, c_range, :],
+                    in_=acc[m][:].rearrange("p (n c) -> p c n", n=TOKENS)[:, c_range, :],
+                )
+                nc.sync.dma_start(
+                    out=out[m * M_TILE : (m + 1) * M_TILE, piece * width * TOKENS : (piece + 1) * width * TOKENS],
+                    in_=out_rows[:, c_range, :].rearrange("p c n -> p (c n)"),
+                )

@@ -26,8 +26,8 @@ RUN = 4
 
 PE_COLS = 192
 PE_SPLIT = 2
-Z_SCALAR_COLS = 64
-LAST_ORDER = (2, 3, 0, 1)
+Z_SCALAR_COLS = 96
+LAST_ORDER = (2, 3, 1, 0)
 STAGE_BUFS = 3
 
 RAW_BUFS = 8
@@ -80,8 +80,9 @@ def tile_attention_pa_k_kernel(tc, y_attn, w_proj, b_proj, grad_out, out):
             nc.sync.dma_start(out=g_raw[:].rearrange("p j w -> p (j w)"), in_=g_passes[k])
             g_grouped = work.tile([P, WIDTH, PACK], BF16, align_bytes=64)
             g_bank = stage.tile([P, PE_COLS, PACK], BF16)
-            step = PE_COLS // PE_SPLIT
-            for s in range(PE_SPLIT):
+            pe_cols = PE_COLS if k < PASSES - 1 else M_TILE
+            step = PE_COLS // PE_SPLIT if k < PASSES - 1 else M_TILE
+            for s in range(pe_cols // step):
                 nc.tensor.matmul(
                     out=g_bank[:, s * step : (s + 1) * step, :],
                     lhsT=ident[:],
@@ -94,7 +95,7 @@ def tile_attention_pa_k_kernel(tc, y_attn, w_proj, b_proj, grad_out, out):
             else:
                 for m in LAST_ORDER[:2]:
                     strided_g(nc.scalar.copy, g_grouped, g_raw, slice(m * M_TILE, (m + 1) * M_TILE))
-            nc.scalar.copy(out=g_grouped[:, :PE_COLS, :], in_=g_bank[:])
+            nc.scalar.copy(out=g_grouped[:, :pe_cols, :], in_=g_bank[:, :pe_cols, :])
             g_grouped_of[k] = (g_grouped, g_raw)
 
         def quantise_z(k):
@@ -137,15 +138,19 @@ def tile_attention_pa_k_kernel(tc, y_attn, w_proj, b_proj, grad_out, out):
         for k in range(PASSES):
             regroup_z(k)
             regroup_g(k)
-            if k > 0:
+            if 0 < k < PASSES - 1:
                 quantise_g(k - 1, slice(0, WIDTH))
                 for m in range(M_TILES):
+                    multiply(k - 1, m)
+            elif k == PASSES - 1:
+                for m in range(M_TILES):
+                    quantise_g(k - 1, slice(m * M_TILE, (m + 1) * M_TILE))
                     multiply(k - 1, m)
             quantise_z(k)
 
         last = PASSES - 1
         g_grouped, g_raw = g_grouped_of[last]
-        strided_g(nc.vector.tensor_copy, g_grouped, g_raw, slice(PE_COLS, 2 * M_TILE))
+        strided_g(nc.vector.tensor_copy, g_grouped, g_raw, slice(M_TILE, 2 * M_TILE))
         for m in LAST_ORDER:
             quantise_g(last, slice(m * M_TILE, (m + 1) * M_TILE))
             multiply(last, m)

@@ -26,10 +26,16 @@ RUN = 4
 
 PE_COLS = 192
 PE_SPLIT = 2
-Z_SCALAR_COLS = 96
+Z_SCALAR_COLS = 64
 LAST_ORDER = (2, 3, 1, 0)
 STAGE_BUFS = 3
 
+SUPERS = 4
+GROUPS = 32
+CLASSES = 4
+PAIR = 2
+PAIRED_PASSES = 24
+PAIR_BUFS = 4
 RAW_BUFS = 8
 WORK_BUFS = 3
 
@@ -39,8 +45,10 @@ def tile_attention_pa_k_kernel(tc, y_attn, w_proj, b_proj, grad_out, out):
 
     g_passes = grad_out.rearrange("(k p h) i w -> k p (h i w)", p=P, h=IMAGES_PER_PARTITION)
     y_passes = y_attn.rearrange("(k p h) n w -> k p (h n w)", p=P, h=IMAGES_PER_PARTITION)
+    g_pairs = grad_out.rearrange("(s a c f) i w -> s c a (f i w)", s=SUPERS, a=GROUPS, c=CLASSES)
+    y_pairs = y_attn.rearrange("(s a c f) n w -> s c a (f n w)", s=SUPERS, a=GROUPS, c=CLASSES)
 
-    with tc.tile_pool(name="raw", bufs=RAW_BUFS) as raw, tc.tile_pool(
+    with tc.tile_pool(name="raw", bufs=RAW_BUFS) as raw, tc.tile_pool(name="pairs", bufs=PAIR_BUFS) as pairs, tc.tile_pool(
         name="work", bufs=WORK_BUFS
     ) as work, tc.tile_pool(name="result", bufs=1) as result, tc.psum_pool(
         name="psum", bufs=1
@@ -51,11 +59,24 @@ def tile_attention_pa_k_kernel(tc, y_attn, w_proj, b_proj, grad_out, out):
         g_operands = {}
         z_operands = {}
         z_grouped_of = {}
+        pair_of = {}
         g_grouped_of = {}
 
         def regroup_z(k):
-            y_raw = raw.tile([P, IMAGES_PER_PARTITION, TOKENS, TOKENS, HALF], BF16)
-            nc.sync.dma_start(out=y_raw[:].rearrange("p h n i c -> p (h n i c)"), in_=y_passes[k])
+            pair, e = divmod(k, PAIR)
+            if k >= PAIRED_PASSES:
+                y_tile = raw.tile([P, IMAGES_PER_PARTITION, TOKENS, TOKENS, HALF], BF16)
+                nc.sync.dma_start(out=y_tile[:].rearrange("p h n i c -> p (h n i c)"), in_=y_passes[k])
+                y_raw = y_tile[:]
+            else:
+                if e == 0:
+                    y_pair = pairs.tile([P, PAIR, IMAGES_PER_PARTITION, TOKENS, TOKENS, HALF], BF16)
+                    nc.sync.dma_start(
+                        out=y_pair[:].rearrange("p e h n i c -> p (e h n i c)"),
+                        in_=y_pairs[pair // CLASSES, pair % CLASSES],
+                    )
+                    pair_of["y"] = y_pair
+                y_raw = pair_of["y"][:, e]
             z_grouped = work.tile([P, TOKENS, HALF, PACK], BF16, align_bytes=64)
             for n in range(TOKENS):
                 vector_cols = HALF if n == 0 else HALF - Z_SCALAR_COLS
@@ -76,8 +97,20 @@ def tile_attention_pa_k_kernel(tc, y_attn, w_proj, b_proj, grad_out, out):
             )
 
         def regroup_g(k):
-            g_raw = raw.tile([P, PACK, WIDTH], BF16)
-            nc.sync.dma_start(out=g_raw[:].rearrange("p j w -> p (j w)"), in_=g_passes[k])
+            pair, e = divmod(k, PAIR)
+            if k >= PAIRED_PASSES:
+                g_tile = raw.tile([P, PACK, WIDTH], BF16)
+                nc.sync.dma_start(out=g_tile[:].rearrange("p j w -> p (j w)"), in_=g_passes[k])
+                g_raw = g_tile[:]
+            else:
+                if e == 0:
+                    g_pair = pairs.tile([P, PAIR, PACK, WIDTH], BF16)
+                    nc.sync.dma_start(
+                        out=g_pair[:].rearrange("p e j w -> p (e j w)"),
+                        in_=g_pairs[pair // CLASSES, pair % CLASSES],
+                    )
+                    pair_of["g"] = g_pair
+                g_raw = pair_of["g"][:, e]
             g_grouped = work.tile([P, WIDTH, PACK], BF16, align_bytes=64)
             g_bank = stage.tile([P, PE_COLS, PACK], BF16)
             pe_cols = PE_COLS if k < PASSES - 1 else M_TILE

import concourse.mybir as mybir
from concourse.masks import make_identity

FLOPS = 2 * 16384 * 512 * 512
BYTES = 2 * 16384 * 512 * 2 + 512 * 512 * 4

BF16 = mybir.dt.bfloat16
F32 = mybir.dt.float32
U32 = mybir.dt.uint32
U8 = mybir.dt.uint8
E4M3_X4 = mybir.dt.float8_e4m3fn_x4
E5M2_X4 = mybir.dt.float8_e5m2_x4

P = 128
PACK = 4
K_PASS = P * PACK
IMAGES = 8192
TOKENS = 2
WIDTH = 512
HALF = WIDTH // TOKENS
PASSES = IMAGES * TOKENS // K_PASS
IMAGES_PER_PARTITION = PACK // TOKENS
M_TILE = 128
M_TILES = WIDTH // M_TILE
RUN = 4

PE_COLS = 192
PE_SPLIT = 2
Z_SCALAR_COLS = 64
LAST_ORDER = (2, 3, 1, 0)
STAGE_BUFS = 3

SUPERS = 4
GROUPS = 32
CLASSES = 4
PAIR = 2
PAIRED_PASSES = 24
PAIR_BUFS = 4
RAW_BUFS = 8
WORK_BUFS = 3


def tile_attention_pa_k_kernel(tc, y_attn, w_proj, b_proj, grad_out, out):
    nc = tc.nc

    g_passes = grad_out.rearrange("(k p h) i w -> k p (h i w)", p=P, h=IMAGES_PER_PARTITION)
    y_passes = y_attn.rearrange("(k p h) n w -> k p (h n w)", p=P, h=IMAGES_PER_PARTITION)
    g_pairs = grad_out.rearrange("(s a c f) i w -> s c a (f i w)", s=SUPERS, a=GROUPS, c=CLASSES)
    y_pairs = y_attn.rearrange("(s a c f) n w -> s c a (f n w)", s=SUPERS, a=GROUPS, c=CLASSES)

    with tc.tile_pool(name="raw", bufs=RAW_BUFS) as raw, tc.tile_pool(name="pairs", bufs=PAIR_BUFS) as pairs, tc.tile_pool(
        name="work", bufs=WORK_BUFS
    ) as work, tc.tile_pool(name="result", bufs=1) as result, tc.psum_pool(
        name="psum", bufs=1
    ) as psum, tc.psum_pool(name="stage", bufs=STAGE_BUFS) as stage, tc.manual_schedule():
        ident = result.tile([P, P], BF16, name="ident")
        make_identity(nc, ident[:])
        acc = [psum.tile([M_TILE, WIDTH], F32, name="acc%d" % m) for m in range(M_TILES)]
        g_operands = {}
        z_operands = {}
        z_grouped_of = {}
        pair_of = {}
        g_grouped_of = {}

        def regroup_z(k):
            pair, e = divmod(k, PAIR)
            if k >= PAIRED_PASSES:
                y_tile = raw.tile([P, IMAGES_PER_PARTITION, TOKENS, TOKENS, HALF], BF16)
                nc.sync.dma_start(out=y_tile[:].rearrange("p h n i c -> p (h n i c)"), in_=y_passes[k])
                y_raw = y_tile[:]
            else:
                if e == 0:
                    y_pair = pairs.tile([P, PAIR, IMAGES_PER_PARTITION, TOKENS, TOKENS, HALF], BF16)
                    nc.sync.dma_start(
                        out=y_pair[:].rearrange("p e h n i c -> p (e h n i c)"),
                        in_=y_pairs[pair // CLASSES, pair % CLASSES],
                    )
                    pair_of["y"] = y_pair
                y_raw = pair_of["y"][:, e]
            z_grouped = work.tile([P, TOKENS, HALF, PACK], BF16, align_bytes=64)
            for n in range(TOKENS):
                vector_cols = HALF if n == 0 else HALF - Z_SCALAR_COLS
                nc.vector.tensor_copy(
                    out=z_grouped[:, n, :vector_cols].rearrange("p (c r) (h i) -> p c h i r", r=RUN, i=TOKENS),
                    in_=y_raw[:, :, n, :, :vector_cols].rearrange("p h i (c r) -> p c h i r", r=RUN),
                )
            nc.scalar.copy(
                out=z_grouped[:, 1, HALF - Z_SCALAR_COLS :].rearrange("p (c r) (h i) -> p c h i r", r=RUN, i=TOKENS),
                in_=y_raw[:, :, 1, :, HALF - Z_SCALAR_COLS :].rearrange("p h i (c r) -> p c h i r", r=RUN),
            )
            z_grouped_of[k] = z_grouped

        def strided_g(copy, g_grouped, g_raw, cols):
            copy(
                out=g_grouped[:, cols, :].rearrange("p (c r) j -> p c j r", r=RUN),
                in_=g_raw[:, :, cols].rearrange("p j (c r) -> p c j r", r=RUN),
            )

        def regroup_g(k):
            pair, e = divmod(k, PAIR)
            if k >= PAIRED_PASSES:
                g_tile = raw.tile([P, PACK, WIDTH], BF16)
                nc.sync.dma_start(out=g_tile[:].rearrange("p j w -> p (j w)"), in_=g_passes[k])
                g_raw = g_tile[:]
            else:
                if e == 0:
                    g_pair = pairs.tile([P, PAIR, PACK, WIDTH], BF16)
                    nc.sync.dma_start(
                        out=g_pair[:].rearrange("p e j w -> p (e j w)"),
                        in_=g_pairs[pair // CLASSES, pair % CLASSES],
                    )
                    pair_of["g"] = g_pair
                g_raw = pair_of["g"][:, e]
            g_grouped = work.tile([P, WIDTH, PACK], BF16, align_bytes=64)
            g_bank = stage.tile([P, PE_COLS, PACK], BF16)
            pe_cols = PE_COLS if k < PASSES - 1 else M_TILE
            step = PE_COLS // PE_SPLIT if k < PASSES - 1 else M_TILE
            for s in range(pe_cols // step):
                nc.tensor.matmul(
                    out=g_bank[:, s * step : (s + 1) * step, :],
                    lhsT=ident[:],
                    rhs=g_raw[:, :, s * step : (s + 1) * step].rearrange("p j c -> p c j"),
                    start=True,
                    stop=True,
                )
            if k < PASSES - 1:
                strided_g(nc.scalar.copy, g_grouped, g_raw, slice(PE_COLS, WIDTH))
            else:
                for m in LAST_ORDER[:2]:
                    strided_g(nc.scalar.copy, g_grouped, g_raw, slice(m * M_TILE, (m + 1) * M_TILE))
            nc.scalar.copy(out=g_grouped[:, :pe_cols, :], in_=g_bank[:, :pe_cols, :])
            g_grouped_of[k] = (g_grouped, g_raw)

        def quantise_z(k):
            z_grouped = z_grouped_of.pop(k)
            z_codes = work.tile([P, WIDTH], U32, align_bytes=64)
            z_scales = work.tile([P, WIDTH], U8, align_bytes=64)
            nc.vector.quantize_mx(
                out=z_codes[:].bitcast(E4M3_X4),
                scales=z_scales[:],
                in_=z_grouped[:].rearrange("p n c j -> p (n c j)"),
            )
            z_operands[k] = (z_codes, z_scales)

        def quantise_g(k, cols):
            if k not in g_operands:
                g_codes = work.tile([P, WIDTH], U32, align_bytes=64)
                g_scales = work.tile([P, WIDTH], U8, align_bytes=64)
                g_operands[k] = (g_codes, g_scales)
            g_codes, g_scales = g_operands[k]
            nc.vector.quantize_mx(
                out=g_codes[:, cols].bitcast(E5M2_X4),
                scales=g_scales[:, cols],
                in_=g_grouped_of[k][0][:, cols, :].rearrange("p w j -> p (w j)"),
            )

        def multiply(k, m):
            z_codes, z_scales = z_operands[k]
            g_codes, g_scales = g_operands[k]
            m_cols = slice(m * M_TILE, (m + 1) * M_TILE)
            nc.tensor.matmul_mx(
                out=acc[m][:],
                lhsT=g_codes[:, m_cols].bitcast(E5M2_X4),
                lhsT_scale=g_scales[:, m_cols],
                rhs=z_codes[:].bitcast(E4M3_X4),
                rhs_scale=z_scales[:],
                start=(k == 0),
                stop=(k == PASSES - 1),
            )

        for k in range(PASSES):
            regroup_z(k)
            regroup_g(k)
            if 0 < k < PASSES - 1:
                quantise_g(k - 1, slice(0, WIDTH))
                for m in range(M_TILES):
                    multiply(k - 1, m)
            elif k == PASSES - 1:
                for m in range(M_TILES):
                    quantise_g(k - 1, slice(m * M_TILE, (m + 1) * M_TILE))
                    multiply(k - 1, m)
            quantise_z(k)

        last = PASSES - 1
        g_grouped, g_raw = g_grouped_of[last]
        strided_g(nc.vector.tensor_copy, g_grouped, g_raw, slice(M_TILE, 2 * M_TILE))
        for m in LAST_ORDER:
            quantise_g(last, slice(m * M_TILE, (m + 1) * M_TILE))
            multiply(last, m)

        for place, m in enumerate(LAST_ORDER):
            out_rows = result.tile([M_TILE, HALF, TOKENS], F32, name="out_rows%d" % m)
            copy_engine = nc.vector.tensor_copy if place % 2 == 0 else nc.scalar.copy
            pieces = 2 if place == M_TILES - 1 else 1
            width = HALF // pieces
            for piece in range(pieces):
                c_range = slice(piece * width, (piece + 1) * width)
                copy_engine(
                    out=out_rows[:, c_range, :],
                    in_=acc[m][:].rearrange("p (n c) -> p c n", n=TOKENS)[:, c_range, :],
                )
                nc.sync.dma_start(
                    out=out[m * M_TILE : (m + 1) * M_TILE, piece * width * TOKENS : (piece + 1) * width * TOKENS],
                    in_=out_rows[:, c_range, :].rearrange("p c n -> p (c n)"),
                )
